import numpy as np
import ml_dtypes


def mxq(x, axis, fmt="e4m3"):
    dtype, down = {"e4m3": (ml_dtypes.float8_e4m3fn, 7), "e5m2": (ml_dtypes.float8_e5m2, 14)}[fmt]
    v = np.moveaxis(np.asarray(x, np.float32).astype(ml_dtypes.bfloat16).astype(np.float64), axis, -1)
    blocks = v.reshape(v.shape[:-1] + (-1, 32))
    amax = np.abs(blocks).max(-1, keepdims=True)
    byte = np.maximum(np.where(amax > 0, np.frexp(amax)[1] - 1 + 127, 0) - down, 1)
    scale = np.exp2(byte - 127.0)
    codes = (blocks / scale).astype(np.float32).astype(dtype).astype(np.float64)
    return np.moveaxis((codes * scale).reshape(v.shape), -1, axis)


WIDE = False


def mx_kscale(k):
    if not WIDE:
        return np.ones(k)
    levels = np.array([20, -20, 10, -10, 0])
    a = np.random.permutation(np.resize(levels, k // 512 * 4)).reshape(k // 512, 4)
    idx = np.arange(k)
    return np.exp2(a[idx // 512, idx % 128 // 32])


BF16 = ml_dtypes.bfloat16


def bf(x):
    return np.asarray(x, np.float32).astype(BF16)


def f64(x):
    return np.asarray(x).astype(np.float64)


K1, K2 = 3, 3
DIL = 1
PAD = (DIL * (K1 - 1) // 2, DIL * (K2 - 1) // 2)
B, CIN, COUT, H, W = 2, 512, 512, 32, 32


def setup_inputs():
    u = mx_kscale(COUT)
    x = np.random.standard_normal((B, CIN, H, W))
    mask = np.random.random((1, K1 * K2, H * W))
    weight = np.random.standard_normal((COUT, CIN, K1, K2)) * 0.03 / u[:, None, None, None]
    bias = np.random.standard_normal(COUT) * 0.5
    g = np.random.standard_normal((B, COUT, H, W)) * np.exp2(np.random.randint(-12, 1, (B, 1, H, W))) * 4.0 * u[None, :, None, None]
    return {"x": bf(x), "mask": bf(mask), "weight": bf(weight), "bias": bf(bias), "grad_out": bf(g)}


def reference(x, mask, weight, bias, grad_out):
    mask, weight, g = f64(mask), f64(weight), f64(grad_out)
    b, cout, h, w = g.shape
    cin = weight.shape[1]
    kk = K1 * K2
    gq = mxq(g.reshape(b, cout, h * w), 1, "e5m2")
    wq = mxq(weight.reshape(cout, cin * kk), 0, "e4m3")
    gp = wq.T @ gq
    gp = gp.reshape(b, cin, kk, h * w) * mask[:, None, :, :]
    gp = gp.reshape(b, cin, kk, h, w)
    p0, p1 = PAD
    gxp = np.zeros((b, cin, h + 2 * p0, w + 2 * p1))
    for i in range(K1):
        for j in range(K2):
            gxp[:, :, i * DIL:i * DIL + h, j * DIL:j * DIL + w] += gp[:, :, i * K2 + j]
    return gxp[:, :, p0:p0 + h, p1:p1 + w]

@@ -1,0 +1,216 @@
+from contextlib import ExitStack
+
+import concourse.bass as bass
+import concourse.mybir as mybir
+import concourse.tile as tile
+from concourse.masks import make_identity
+
+F32 = mybir.dt.float32
+BF16 = mybir.dt.bfloat16
+U32 = mybir.dt.uint32
+U8 = mybir.dt.uint8
+I32 = mybir.dt.int32
+E4 = mybir.dt.float8_e4m3fn_x4
+E5 = mybir.dt.float8_e5m2_x4
+ALU = mybir.AluOpType
+ACT = mybir.ActivationFunctionType
+
+P = 128
+B, CIN, COUT, H, W = 2, 512, 512, 32, 32
+L = H * W
+TAPS = 9
+NBLK = 16
+GCOLS = 64 * (H + 2)
+FLOPS = 2 * COUT * CIN * TAPS * B * L
+BYTES = 2 * (COUT * CIN * TAPS + B * COUT * L + TAPS * L) + 4 * B * CIN * L
+
+DZ_ORDER = (0, 1, -1)
+GROUPS = (tuple(range(0, 8)), tuple(range(8, 16)))
+S_SHARE = 34
+
+
+def tile_input_masked_conv2d_kernel(tc, x, mask, weight, bias, grad_out, out):
+    nc = tc.nc
+    with ExitStack() as ctx:
+        keep = ctx.enter_context(tc.tile_pool(name="keep", bufs=1))
+        wgp = ctx.enter_context(tc.tile_pool(name="wgp", bufs=4))
+        gsp = ctx.enter_context(tc.tile_pool(name="gsp", bufs=2))
+        tmpp = ctx.enter_context(tc.tile_pool(name="tmpp", bufs=4))
+        otp = ctx.enter_context(tc.tile_pool(name="otp", bufs=3))
+        psum = ctx.enter_context(tc.psum_pool(name="psum", bufs=6))
+        psum_t = ctx.enter_context(tc.psum_pool(name="psum_t", bufs=2))
+
+        ms = keep.tile([P, L], BF16, name="ms")
+        nc.vector.memset(ms[:], 0.0)
+        mflat = mask.rearrange("a t l -> a (t l)")
+        for tap in range(TAPS):
+            shift = 32 * (1 - tap // 3) + (1 - tap % 3)
+            lo = tap * L + shift
+            nc.gpsimd.dma_start(out=ms[tap : tap + 1, :], in_=mflat[:, lo : lo + L])
+
+        graw = keep.tile([P, B, 4, L], BF16, name="graw")
+        for b in range(B):
+            nc.sync.dma_start(out=graw[:, b], in_=grad_out[b].rearrange("(p j) y z -> p j (y z)", j=4))
+        wview = weight.rearrange("(p j) c i k -> p j (c i k)", j=4)
+        wraw = []
+        for q in range(4):
+            wr = keep.tile([P, 4, 128 * TAPS], BF16, name="wraw%d" % q)
+            nc.sync.dma_start(out=wr[:], in_=wview[:, :, q * 1152 : (q + 1) * 1152])
+            wraw.append(wr)
+
+        ident = keep.tile([P, P], F32, name="ident")
+        make_identity(nc, ident[:])
+        perm = keep.tile([P, P], F32, name="perm")
+        nc.vector.tensor_copy(
+            out=perm[:].rearrange("p (b d z) -> p b d z", b=2, d=2),
+            in_=ident[:].rearrange("p (d b z) -> p b d z", b=2, d=2),
+        )
+
+        gcodes = {}
+        gsc = {}
+        for dz in DZ_ORDER:
+            gc = keep.tile([P, GCOLS], U32, name="gcodes%d" % (dz + 1), align_bytes=64)
+            gs_ = keep.tile([P, GCOLS], U8, name="gsc%d" % (dz + 1), align_bytes=64)
+            for c0 in (0, GCOLS - 64):
+                nc.vector.memset(gc[:, c0 : c0 + 64].bitcast(I32), 0)
+                nc.vector.memset(gs_[:, c0 : c0 + 64].bitcast(I32), 0)
+            gcodes[dz] = gc
+            gsc[dz] = gs_
+        wcodes = keep.tile([P, TAPS * CIN], U32, name="wcodes", align_bytes=64)
+        wsc = keep.tile([P, TAPS * CIN], U8, name="wsc", align_bytes=64)
+
+        msd = keep.tile([P, NBLK * P], F32, name="msd")
+        nc.vector.tensor_copy(
+            out=msd[:].rearrange("k (y b z) -> k y b z", b=2, z=32),
+            in_=ms[:].rearrange("k (y z) -> k y z", z=32).unsqueeze(2).to_broadcast([P, H, 2, W]),
+        )
+        maskp = keep.tile([P, NBLK, TAPS], F32, name="maskp")
+        for g in range(4):
+            tpm = psum_t.tile([P, 4, P], F32, tag="tp", name="tpm")
+            for u in range(4):
+                yb = 4 * g + u
+                nc.tensor.transpose(tpm[:, u, :], msd[:, yb * P : (yb + 1) * P], ident[:])
+            nc.vector.tensor_copy(out=maskp[:, 4 * g : 4 * g + 4, :], in_=tpm[:, :, 0:TAPS])
+
+        gg0 = keep.tile([P, 4 * B * L], BF16, name="gg0", align_bytes=64)
+        gg0v = gg0[:].rearrange("p (y b z j) -> p y b z j", b=2, z=32, j=4)
+        grawv = graw[:].rearrange("p b j (y z) -> p y b z j", z=32)
+
+        def g_regroup(eng_copy, b, h):
+            eng_copy(out=gg0v[:, 16 * h : 16 * h + 16, b], in_=grawv[:, 16 * h : 16 * h + 16, b])
+
+        def g_quant(dz, h, src):
+            nc.vector.quantize_mx(
+                out=gcodes[dz][:, 64 + 1024 * h : 64 + 1024 * (h + 1)].bitcast(E5),
+                scales=gsc[dz][:, 64 + 1024 * h : 64 + 1024 * (h + 1)],
+                in_=src,
+            )
+
+        def g_prep(dz):
+            if dz == 0:
+                g_regroup(nc.vector.tensor_copy, 0, 0)
+                g_regroup(nc.vector.tensor_copy, 0, 1)
+                g_regroup(nc.scalar.copy, 1, 0)
+                g_regroup(nc.vector.tensor_copy, 1, 1)
+                for h in range(2):
+                    g_quant(0, h, gg0[:, 4096 * h : 4096 * (h + 1)])
+                return
+            shifted = []
+            for h in range(2):
+                gs = gsp.tile([P, 4096], BF16, tag="gs", name="gs", align_bytes=64)
+                if dz == 1:
+                    nc.vector.tensor_copy(out=gs[:, 0:4092], in_=gg0[:, 4096 * h + 4 : 4096 * (h + 1)])
+                    edge = 31
+                else:
+                    nc.vector.tensor_copy(out=gs[:, 4:4096], in_=gg0[:, 4096 * h : 4096 * (h + 1) - 4])
+                    edge = 0
+                nc.vector.memset(gs[:].rearrange("p (g z j) -> p g z j", z=32, j=4)[:, :, edge, :], 0.0)
+                shifted.append(gs)
+            for h in range(2):
+                g_quant(dz, h, shifted[h][:])
+
+        def w_prep(dz, engines):
+            k = 1 - dz
+            for q in range(4):
+                wg = wgp.tile([P, 3, 128, 4], BF16, tag="wg", name="wg", align_bytes=64)
+                engines[q](
+                    out=wg[:].rearrange("p t c j -> p c t j"),
+                    in_=wraw[q][:].rearrange("p j (c i k) -> p c i k j", i=3, k=3)[:, :, :, k, :],
+                )
+                for t in range(3):
+                    tap = 3 * t + k
+                    c0 = tap * CIN + q * 128
+                    nc.vector.quantize_mx(
+                        out=wcodes[:, c0 : c0 + 128].bitcast(E4),
+                        scales=wsc[:, c0 : c0 + 128],
+                        in_=wg[:, t].rearrange("p c j -> p (c j)"),
+                    )
+
+        acc = {}
+        state = {"n": 0}
+
+        def one_bank(yb, tap, first):
+            dy, dz = 1 - tap // 3, 1 - tap % 3
+            c0 = 64 + (2 * yb + dy) * 64
+            ps = psum.tile([P, CIN], F32, tag="mx", name="ps")
+            nc.tensor.matmul_mx(
+                out=ps[:],
+                lhsT=gcodes[dz][:, c0 : c0 + P].bitcast(E5),
+                lhsT_scale=gsc[dz][:, c0 : c0 + P],
+                rhs=wcodes[:, tap * CIN : (tap + 1) * CIN].bitcast(E4),
+                rhs_scale=wsc[:, tap * CIN : (tap + 1) * CIN],
+                start=True,
+                stop=True,
+            )
+            m = maskp[:, yb, tap : tap + 1]
+            if first:
+                a = keep.tile([P, CIN], F32, name="acc%d" % yb)
+                acc[yb] = a
+                nc.scalar.activation(out=a[:], in_=ps[:], func=ACT.Copy, scale=m)
+                return
+            a = acc[yb]
+            n = state["n"]
+            state["n"] = n + 1
+            if (n * S_SHARE) % 100 < S_SHARE:
+                t = tmpp.tile([P, CIN], F32, tag="tmp", name="tmp")
+                nc.scalar.activation(out=t[:], in_=ps[:], func=ACT.Copy, scale=m)
+                nc.gpsimd.tensor_tensor(out=a[:], in0=a[:], in1=t[:], op=ALU.add)
+            else:
+                nc.vector.scalar_tensor_tensor(
+                    out=a[:], in0=ps[:], scalar=m, in1=a[:], op0=ALU.mult, op1=ALU.add
+                )
+
+        def finish_pair(pr):
+            ot = otp.tile([P, 4, 2, P], F32, tag="ot", name="ot")
+            for hh in range(2):
+                yb = 2 * pr + hh
+                tp = psum_t.tile([P, 4, P], F32, tag="tp", name="tp")
+                for cb in range(4):
+                    nc.tensor.transpose(tp[:, cb, :], acc[yb][:, cb * P : (cb + 1) * P], perm[:])
+                nc.scalar.copy(
+                    out=ot[:, :, :, 64 * hh : 64 * hh + 64],
+                    in_=tp[:].rearrange("p cb (b r) -> p cb b r", b=2),
+                )
+            for b in range(B):
+                nc.sync.dma_start(
+                    out=out[b].rearrange("(cb c) y z -> c cb (y z)", c=P)[:, :, pr * P : (pr + 1) * P],
+                    in_=ot[:, :, b, :],
+                )
+
+        vcopy = nc.vector.tensor_copy
+        scopy = nc.scalar.copy
+        g_prep(0)
+        w_prep(0, (scopy, scopy, scopy, scopy))
+        g_prep(1)
+        w_prep(1, (vcopy, scopy, vcopy, scopy))
+        for gi, group in enumerate(GROUPS):
+            for ph, dz in enumerate(DZ_ORDER):
+                if gi == 0 and ph == 1:
+                    g_prep(-1)
+                    w_prep(-1, (vcopy, scopy, vcopy, scopy))
+                for t in range(3):
+                    tap = 3 * t + (1 - dz)
+                    for yb in group:
+                        one_bank(yb, tap, ph == 0 and t == 0)
+            for pr in range(group[0] // 2, group[-1] // 2 + 1):
+                finish_pair(pr)

@@ -24,9 +24,12 @@ GCOLS = 64 * (H + 2)
 FLOPS = 2 * COUT * CIN * TAPS * B * L
 BYTES = 2 * (COUT * CIN * TAPS + B * COUT * L + TAPS * L) + 4 * B * CIN * L
 
-DZ_ORDER = (0, 1, -1)
-GROUPS = (tuple(range(0, 8)), tuple(range(8, 16)))
-S_SHARE = 34
+K_ORDER = (1, 0, 2)
+COPIES = (0, 2)
+CHAIN = {0: 0, 1: 0, 2: 0}
+W_ENG = {1: "SSSS", 0: "SSSS", 2: "VVVV"}
+T_V, T_S, T_G, T_PASS, T_TILE, T_OUT = 0.487, 0.53, 0.95, 0.225, 0.264, 0.45
+G_SLACK = 4.0
 
 
 def tile_input_masked_conv2d_kernel(tc, x, mask, weight, bias, grad_out, out):
@@ -37,6 +40,7 @@ def tile_input_masked_conv2d_kernel(tc, x, mask, weight, bias, grad_out, out):
         gsp = ctx.enter_context(tc.tile_pool(name="gsp", bufs=2))
         tmpp = ctx.enter_context(tc.tile_pool(name="tmpp", bufs=4))
         otp = ctx.enter_context(tc.tile_pool(name="otp", bufs=3))
+        accp = ctx.enter_context(tc.tile_pool(name="accp", bufs=20))
         psum = ctx.enter_context(tc.psum_pool(name="psum", bufs=6))
         psum_t = ctx.enter_context(tc.psum_pool(name="psum_t", bufs=2))
 
@@ -44,9 +48,18 @@ def tile_input_masked_conv2d_kernel(tc, x, mask, weight, bias, grad_out, out):
         nc.vector.memset(ms[:], 0.0)
         mflat = mask.rearrange("a t l -> a (t l)")
         for tap in range(TAPS):
-            shift = 32 * (1 - tap // 3) + (1 - tap % 3)
-            lo = tap * L + shift
-            nc.gpsimd.dma_start(out=ms[tap : tap + 1, :], in_=mflat[:, lo : lo + L])
+            k = tap % 3
+            dz = 1 - k
+            if k in COPIES or dz == 0:
+                lo = tap * L + 32 * (1 - tap // 3) + dz
+                nc.gpsimd.dma_start(out=ms[tap : tap + 1, :], in_=mflat[:, lo : lo + L])
+            else:
+                lo = tap * L + 32 * (1 - tap // 3)
+                z0 = 1 if dz == 1 else 0
+                nc.gpsimd.dma_start(
+                    out=ms[tap : tap + 1, :].rearrange("o (y z) -> o y z", z=32)[:, :, z0 : z0 + 31],
+                    in_=mflat[:, lo : lo + L].rearrange("a (y z) -> a y z", z=32)[:, :, z0 : z0 + 31],
+                )
 
         graw = keep.tile([P, B, 4, L], BF16, name="graw")
         for b in range(B):
@@ -60,29 +73,45 @@ def tile_input_masked_conv2d_kernel(tc, x, mask, weight, bias, grad_out, out):
 
         ident = keep.tile([P, P], F32, name="ident")
         make_identity(nc, ident[:])
-        perm = keep.tile([P, P], F32, name="perm")
-        nc.vector.tensor_copy(
-            out=perm[:].rearrange("p (b d z) -> p b d z", b=2, d=2),
-            in_=ident[:].rearrange("p (d b z) -> p b d z", b=2, d=2),
-        )
+        iv = ident[:].rearrange("p (d b z) -> p b d z", b=2, d=2)
+        perms = {}
+        for k in K_ORDER:
+            dz = 0 if k in COPIES else 1 - k
+            if dz in perms:
+                continue
+            pm = keep.tile([P, P], F32, name="perm%d" % (dz + 1))
+            pv = pm[:].rearrange("p (b d z) -> p b d z", b=2, d=2)
+            if dz == 0:
+                nc.vector.tensor_copy(out=pv, in_=iv)
+            elif dz == 1:
+                nc.vector.tensor_copy(out=pv[:, :, :, 0:31], in_=iv[:, :, :, 1:32])
+                nc.vector.tensor_copy(out=pv[:, :, :, 31:32], in_=iv[:, :, :, 0:1])
+            else:
+                nc.vector.tensor_copy(out=pv[:, :, :, 1:32], in_=iv[:, :, :, 0:31])
+                nc.vector.tensor_copy(out=pv[:, :, :, 0:1], in_=iv[:, :, :, 31:32])
+            perms[dz] = pm
 
         gcodes = {}
         gsc = {}
-        for dz in DZ_ORDER:
-            gc = keep.tile([P, GCOLS], U32, name="gcodes%d" % (dz + 1), align_bytes=64)
-            gs_ = keep.tile([P, GCOLS], U8, name="gsc%d" % (dz + 1), align_bytes=64)
+        for k in (1,) + COPIES:
+            gc = keep.tile([P, GCOLS], U32, name="gcodes%d" % k, align_bytes=64)
+            gs_ = keep.tile([P, GCOLS], U8, name="gsc%d" % k, align_bytes=64)
             for c0 in (0, GCOLS - 64):
                 nc.vector.memset(gc[:, c0 : c0 + 64].bitcast(I32), 0)
                 nc.vector.memset(gs_[:, c0 : c0 + 64].bitcast(I32), 0)
-            gcodes[dz] = gc
-            gsc[dz] = gs_
+            gcodes[k] = gc
+            gsc[k] = gs_
         wcodes = keep.tile([P, TAPS * CIN], U32, name="wcodes", align_bytes=64)
         wsc = keep.tile([P, TAPS * CIN], U8, name="wsc", align_bytes=64)
 
         msd = keep.tile([P, NBLK * P], F32, name="msd")
-        nc.vector.tensor_copy(
+        nc.gpsimd.tensor_scalar(
             out=msd[:].rearrange("k (y b z) -> k y b z", b=2, z=32),
-            in_=ms[:].rearrange("k (y z) -> k y z", z=32).unsqueeze(2).to_broadcast([P, H, 2, W]),
+            in0=ms[:].rearrange("k (y z) -> k y z", z=32).unsqueeze(2).to_broadcast([P, H, 2, W]),
+            scalar1=1.0,
+            scalar2=0.0,
+            op0=ALU.mult,
+            op1=ALU.add,
         )
         maskp = keep.tile([P, NBLK, TAPS], F32, name="maskp")
         for g in range(4):
@@ -99,26 +128,26 @@ def tile_input_masked_conv2d_kernel(tc, x, mask, weight, bias, grad_out, out):
         def g_regroup(eng_copy, b, h):
             eng_copy(out=gg0v[:, 16 * h : 16 * h + 16, b], in_=grawv[:, 16 * h : 16 * h + 16, b])
 
-        def g_quant(dz, h, src):
+        def g_quant(k, h, src):
             nc.vector.quantize_mx(
-                out=gcodes[dz][:, 64 + 1024 * h : 64 + 1024 * (h + 1)].bitcast(E5),
-                scales=gsc[dz][:, 64 + 1024 * h : 64 + 1024 * (h + 1)],
+                out=gcodes[k][:, 64 + 1024 * h : 64 + 1024 * (h + 1)].bitcast(E5),
+                scales=gsc[k][:, 64 + 1024 * h : 64 + 1024 * (h + 1)],
                 in_=src,
             )
 
-        def g_prep(dz):
-            if dz == 0:
+        def g_prep(k):
+            if k == 1:
                 g_regroup(nc.vector.tensor_copy, 0, 0)
                 g_regroup(nc.vector.tensor_copy, 0, 1)
                 g_regroup(nc.scalar.copy, 1, 0)
                 g_regroup(nc.vector.tensor_copy, 1, 1)
                 for h in range(2):
-                    g_quant(0, h, gg0[:, 4096 * h : 4096 * (h + 1)])
+                    g_quant(1, h, gg0[:, 4096 * h : 4096 * (h + 1)])
                 return
             shifted = []
             for h in range(2):
                 gs = gsp.tile([P, 4096], BF16, tag="gs", name="gs", align_bytes=64)
-                if dz == 1:
+                if k == 0:
                     nc.vector.tensor_copy(out=gs[:, 0:4092], in_=gg0[:, 4096 * h + 4 : 4096 * (h + 1)])
                     edge = 31
                 else:
@@ -127,90 +156,141 @@ def tile_input_masked_conv2d_kernel(tc, x, mask, weight, bias, grad_out, out):
                 nc.vector.memset(gs[:].rearrange("p (g z j) -> p g z j", z=32, j=4)[:, :, edge, :], 0.0)
                 shifted.append(gs)
             for h in range(2):
-                g_quant(dz, h, shifted[h][:])
+                g_quant(k, h, shifted[h][:])
 
-        def w_prep(dz, engines):
-            k = 1 - dz
+        load = {"V": 4.0, "S": 4.0, "G": 10.0, "PE": 8.0}
+
+        def w_prep(k):
             for q in range(4):
                 wg = wgp.tile([P, 3, 128, 4], BF16, tag="wg", name="wg", align_bytes=64)
-                engines[q](
+                if W_ENG[k][q] == "V":
+                    eng_copy = nc.vector.tensor_copy
+                    load["V"] += 0.97
+                else:
+                    eng_copy = nc.scalar.copy
+                    load["S"] += 1.74
+                load["V"] += 0.39
+                eng_copy(
                     out=wg[:].rearrange("p t c j -> p c t j"),
                     in_=wraw[q][:].rearrange("p j (c i k) -> p c i k j", i=3, k=3)[:, :, :, k, :],
                 )
                 for t in range(3):
-                    tap = 3 * t + k
-                    c0 = tap * CIN + q * 128
+                    c0 = (3 * t + k) * CIN + q * 128
                     nc.vector.quantize_mx(
                         out=wcodes[:, c0 : c0 + 128].bitcast(E4),
                         scales=wsc[:, c0 : c0 + 128],
                         in_=wg[:, t].rearrange("p c j -> p (c j)"),
                     )
 
-        acc = {}
-        state = {"n": 0}
+        chains = {}
 
-        def one_bank(yb, tap, first):
-            dy, dz = 1 - tap // 3, 1 - tap % 3
+        def one_bank(yb, tap):
+            dy, k = 1 - tap // 3, tap % 3
+            src = k if k in COPIES else 1
             c0 = 64 + (2 * yb + dy) * 64
             ps = psum.tile([P, CIN], F32, tag="mx", name="ps")
             nc.tensor.matmul_mx(
                 out=ps[:],
-                lhsT=gcodes[dz][:, c0 : c0 + P].bitcast(E5),
-                lhsT_scale=gsc[dz][:, c0 : c0 + P],
+                lhsT=gcodes[src][:, c0 : c0 + P].bitcast(E5),
+                lhsT_scale=gsc[src][:, c0 : c0 + P],
                 rhs=wcodes[:, tap * CIN : (tap + 1) * CIN].bitcast(E4),
                 rhs_scale=wsc[:, tap * CIN : (tap + 1) * CIN],
                 start=True,
                 stop=True,
             )
             m = maskp[:, yb, tap : tap + 1]
-            if first:
-                a = keep.tile([P, CIN], F32, name="acc%d" % yb)
-                acc[yb] = a
+            key = (yb, CHAIN[k])
+            if key not in chains:
+                chains[key] = {"v": None, "s": []}
+            ch = chains[key]
+            load["PE"] += T_PASS
+            ref = max(load["V"], load["S"])
+            how = "V"
+            if load["S"] + T_S <= load["V"] + T_V:
+                room = load["PE"] + T_TILE <= ref
+                if not ch["s"] and (ch["v"] is None or room):
+                    how = "S"
+                elif ch["s"] and max(load["G"], load["S"] + T_S) + T_G <= ref + G_SLACK:
+                    how = "G"
+                elif room:
+                    how = "S"
+            if how == "V":
+                load["V"] += T_V
+                if ch["v"] is not None:
+                    a = ch["v"]
+                    nc.vector.scalar_tensor_tensor(out=a[:], in0=ps[:], scalar=m, in1=a[:], op0=ALU.mult, op1=ALU.add)
+                elif ch["s"]:
+                    a = ch["s"].pop()
+                    ch["v"] = a
+                    nc.vector.scalar_tensor_tensor(out=a[:], in0=ps[:], scalar=m, in1=a[:], op0=ALU.mult, op1=ALU.add)
+                else:
+                    a = accp.tile([P, CIN], F32, tag="acc", name="acc")
+                    ch["v"] = a
+                    load["PE"] += T_TILE
+                    nc.vector.tensor_scalar(out=a[:], in0=ps[:], scalar1=m, scalar2=None, op0=ALU.mult)
+            elif how == "S":
+                load["S"] += T_S
+                load["PE"] += T_TILE
+                a = accp.tile([P, CIN], F32, tag="acc", name="acc")
+                ch["s"].append(a)
                 nc.scalar.activation(out=a[:], in_=ps[:], func=ACT.Copy, scale=m)
-                return
-            a = acc[yb]
-            n = state["n"]
-            state["n"] = n + 1
-            if (n * S_SHARE) % 100 < S_SHARE:
+            else:
+                load["S"] += T_S
+                load["G"] = max(load["G"], load["S"]) + T_G
+                a = ch["s"][-1]
                 t = tmpp.tile([P, CIN], F32, tag="tmp", name="tmp")
                 nc.scalar.activation(out=t[:], in_=ps[:], func=ACT.Copy, scale=m)
                 nc.gpsimd.tensor_tensor(out=a[:], in0=a[:], in1=t[:], op=ALU.add)
-            else:
-                nc.vector.scalar_tensor_tensor(
-                    out=a[:], in0=ps[:], scalar=m, in1=a[:], op0=ALU.mult, op1=ALU.add
-                )
 
         def finish_pair(pr):
             ot = otp.tile([P, 4, 2, P], F32, tag="ot", name="ot")
+            banks = []
             for hh in range(2):
                 yb = 2 * pr + hh
+                parts = []
+                for k in K_ORDER:
+                    key = (yb, CHAIN[k])
+                    if key in chains:
+                        ch = chains.pop(key)
+                        dz = 0 if k in COPIES else 1 - k
+                        tiles = ([ch["v"]] if ch["v"] is not None else []) + ch["s"]
+                        parts.extend([(a, perms[dz]) for a in tiles])
                 tp = psum_t.tile([P, 4, P], F32, tag="tp", name="tp")
                 for cb in range(4):
-                    nc.tensor.transpose(tp[:, cb, :], acc[yb][:, cb * P : (cb + 1) * P], perm[:])
-                nc.scalar.copy(
-                    out=ot[:, :, :, 64 * hh : 64 * hh + 64],
-                    in_=tp[:].rearrange("p cb (b r) -> p cb b r", b=2),
-                )
+                    for n, (a, pm) in enumerate(parts):
+                        nc.tensor.matmul(
+                            out=tp[:, cb, :],
+                            lhsT=a[:, cb * P : (cb + 1) * P],
+                            rhs=pm[:],
+                            is_transpose=True,
+                            start=(n == 0),
+                            stop=(n == len(parts) - 1),
+                        )
+                banks.append(tp)
+            for hh in range(2):
+                dst = ot[:, :, :, 64 * hh : 64 * hh + 64]
+                src = banks[hh][:].rearrange("p cb (b r) -> p cb b r", b=2)
+                if load["V"] + T_OUT < load["S"]:
+                    load["V"] += T_OUT
+                    nc.vector.tensor_copy(out=dst, in_=src)
+                else:
+                    load["S"] += T_OUT
+                    nc.scalar.copy(out=dst, in_=src)
             for b in range(B):
                 nc.sync.dma_start(
                     out=out[b].rearrange("(cb c) y z -> c cb (y z)", c=P)[:, :, pr * P : (pr + 1) * P],
                     in_=ot[:, :, b, :],
                 )
 
-        vcopy = nc.vector.tensor_copy
-        scopy = nc.scalar.copy
-        g_prep(0)
-        w_prep(0, (scopy, scopy, scopy, scopy))
         g_prep(1)
-        w_prep(1, (vcopy, scopy, vcopy, scopy))
-        for gi, group in enumerate(GROUPS):
-            for ph, dz in enumerate(DZ_ORDER):
-                if gi == 0 and ph == 1:
-                    g_prep(-1)
-                    w_prep(-1, (vcopy, scopy, vcopy, scopy))
+        for k in K_ORDER:
+            if k in COPIES:
+                g_prep(k)
+                load["V"] += 3.84
+            w_prep(k)
+        for pr in range(NBLK // 2):
+            for k in K_ORDER:
                 for t in range(3):
-                    tap = 3 * t + (1 - dz)
-                    for yb in group:
-                        one_bank(yb, tap, ph == 0 and t == 0)
-            for pr in range(group[0] // 2, group[-1] // 2 + 1):
-                finish_pair(pr)
+                    for hh in range(2):
+                        one_bank(2 * pr + hh, 3 * t + k)
+            finish_pair(pr)

@@ -25,45 +25,30 @@ FLOPS = 2 * COUT * CIN * TAPS * B * L
 BYTES = 2 * (COUT * CIN * TAPS + B * COUT * L + TAPS * L) + 4 * B * CIN * L
 
 K_ORDER = (1, 0, 2)
-COPIES = (0, 2)
-CHAIN = {0: 0, 1: 0, 2: 0}
-W_ENG = {1: "SSSS", 0: "SSSS", 2: "VVVV"}
-T_V, T_S, T_G, T_PASS, T_TILE, T_OUT = 0.487, 0.53, 0.95, 0.225, 0.264, 0.45
-G_SLACK = 4.0
+W_ENG = {"0":"SSSS","1":"VVVV","2":"VSVS"}
+PIN = False
 
 
 def tile_input_masked_conv2d_kernel(tc, x, mask, weight, bias, grad_out, out):
     nc = tc.nc
     with ExitStack() as ctx:
+        if PIN:
+            ctx.enter_context(tc.manual_schedule())
         keep = ctx.enter_context(tc.tile_pool(name="keep", bufs=1))
-        wgp = ctx.enter_context(tc.tile_pool(name="wgp", bufs=4))
-        gsp = ctx.enter_context(tc.tile_pool(name="gsp", bufs=2))
-        tmpp = ctx.enter_context(tc.tile_pool(name="tmpp", bufs=4))
         otp = ctx.enter_context(tc.tile_pool(name="otp", bufs=3))
-        accp = ctx.enter_context(tc.tile_pool(name="accp", bufs=20))
+        accp = ctx.enter_context(tc.tile_pool(name="accp", bufs=16))
         psum = ctx.enter_context(tc.psum_pool(name="psum", bufs=6))
         psum_t = ctx.enter_context(tc.psum_pool(name="psum_t", bufs=2))
 
         ms = keep.tile([P, L], BF16, name="ms")
         nc.vector.memset(ms[:], 0.0)
-        mflat = mask.rearrange("a t l -> a (t l)")
-        for tap in range(TAPS):
-            k = tap % 3
-            dz = 1 - k
-            if k in COPIES or dz == 0:
-                lo = tap * L + 32 * (1 - tap // 3) + dz
-                nc.gpsimd.dma_start(out=ms[tap : tap + 1, :], in_=mflat[:, lo : lo + L])
-            else:
-                lo = tap * L + 32 * (1 - tap // 3)
-                z0 = 1 if dz == 1 else 0
-                nc.gpsimd.dma_start(
-                    out=ms[tap : tap + 1, :].rearrange("o (y z) -> o y z", z=32)[:, :, z0 : z0 + 31],
-                    in_=mflat[:, lo : lo + L].rearrange("a (y z) -> a y z", z=32)[:, :, z0 : z0 + 31],
-                )
-
         graw = keep.tile([P, B, 4, L], BF16, name="graw")
         for b in range(B):
             nc.sync.dma_start(out=graw[:, b], in_=grad_out[b].rearrange("(p j) y z -> p j (y z)", j=4))
+        for i in range(3):
+            dy = 1 - i
+            d0, s0, n = max(0, -32 * dy), max(0, 32 * dy), L - 32 * abs(dy)
+            nc.scalar.dma_start(out=ms[i:96:32, d0 : d0 + n], in_=mask[0, 3 * i : 3 * i + 3, s0 : s0 + n])
         wview = weight.rearrange("(p j) c i k -> p j (c i k)", j=4)
         wraw = []
         for q in range(4):
@@ -76,221 +61,151 @@ def tile_input_masked_conv2d_kernel(tc, x, mask, weight, bias, grad_out, out):
         iv = ident[:].rearrange("p (d b z) -> p b d z", b=2, d=2)
         perms = {}
         for k in K_ORDER:
-            dz = 0 if k in COPIES else 1 - k
-            if dz in perms:
-                continue
-            pm = keep.tile([P, P], F32, name="perm%d" % (dz + 1))
+            pm = keep.tile([P, P], F32, name="perm%d" % k)
             pv = pm[:].rearrange("p (b d z) -> p b d z", b=2, d=2)
-            if dz == 0:
+            if k == 1:
                 nc.vector.tensor_copy(out=pv, in_=iv)
-            elif dz == 1:
+            elif k == 0:
                 nc.vector.tensor_copy(out=pv[:, :, :, 0:31], in_=iv[:, :, :, 1:32])
                 nc.vector.tensor_copy(out=pv[:, :, :, 31:32], in_=iv[:, :, :, 0:1])
             else:
                 nc.vector.tensor_copy(out=pv[:, :, :, 1:32], in_=iv[:, :, :, 0:31])
                 nc.vector.tensor_copy(out=pv[:, :, :, 0:1], in_=iv[:, :, :, 31:32])
-            perms[dz] = pm
+            perms[k] = pm
 
-        gcodes = {}
-        gsc = {}
-        for k in (1,) + COPIES:
-            gc = keep.tile([P, GCOLS], U32, name="gcodes%d" % k, align_bytes=64)
-            gs_ = keep.tile([P, GCOLS], U8, name="gsc%d" % k, align_bytes=64)
-            for c0 in (0, GCOLS - 64):
-                nc.vector.memset(gc[:, c0 : c0 + 64].bitcast(I32), 0)
-                nc.vector.memset(gs_[:, c0 : c0 + 64].bitcast(I32), 0)
-            gcodes[k] = gc
-            gsc[k] = gs_
+        gcodes = keep.tile([P, GCOLS], U32, name="gcodes", align_bytes=64)
+        gsc = keep.tile([P, GCOLS], U8, name="gsc", align_bytes=64)
+        for c0 in (0, GCOLS - 64):
+            nc.vector.memset(gcodes[:, c0 : c0 + 64].bitcast(I32), 0)
+            nc.vector.memset(gsc[:, c0 : c0 + 64].bitcast(I32), 0)
         wcodes = keep.tile([P, TAPS * CIN], U32, name="wcodes", align_bytes=64)
         wsc = keep.tile([P, TAPS * CIN], U8, name="wsc", align_bytes=64)
 
+        msv = ms[:].rearrange("r (y z) -> r y z", z=32)
+        nc.gpsimd.memset(msv[0:3, :, 0:1], 0.0)
+        nc.gpsimd.memset(msv[64:67, :, 31:32], 0.0)
         msd = keep.tile([P, NBLK * P], F32, name="msd")
         nc.gpsimd.tensor_scalar(
-            out=msd[:].rearrange("k (y b z) -> k y b z", b=2, z=32),
-            in0=ms[:].rearrange("k (y z) -> k y z", z=32).unsqueeze(2).to_broadcast([P, H, 2, W]),
+            out=msd[:].rearrange("r (y b z) -> r y b z", b=2, z=32),
+            in0=msv.unsqueeze(2).to_broadcast([P, H, 2, W]),
             scalar1=1.0,
             scalar2=0.0,
             op0=ALU.mult,
             op1=ALU.add,
         )
-        maskp = keep.tile([P, NBLK, TAPS], F32, name="maskp")
+
+        gg0 = keep.tile([P, 4 * B * L], BF16, name="gg0", align_bytes=64)
+        gg0v = gg0[:].rearrange("p (y b z j) -> p y b z j", b=2, z=32, j=4)
+        grawv = graw[:].rearrange("p b j (y z) -> p y b z j", z=32)
+        for eng_copy, b, h in (
+            (nc.vector.tensor_copy, 0, 0),
+            (nc.vector.tensor_copy, 0, 1),
+            (nc.scalar.copy, 1, 0),
+            (nc.vector.tensor_copy, 1, 1),
+        ):
+            eng_copy(out=gg0v[:, 16 * h : 16 * h + 16, b], in_=grawv[:, 16 * h : 16 * h + 16, b])
+        for h in range(2):
+            nc.vector.quantize_mx(
+                out=gcodes[:, 64 + 1024 * h : 64 + 1024 * (h + 1)].bitcast(E5),
+                scales=gsc[:, 64 + 1024 * h : 64 + 1024 * (h + 1)],
+                in_=gg0[:, 4096 * h : 4096 * (h + 1)],
+            )
+
+        maskp = keep.tile([P, NBLK, 3, 3], F32, name="maskp")
         for g in range(4):
             tpm = psum_t.tile([P, 4, P], F32, tag="tp", name="tpm")
             for u in range(4):
                 yb = 4 * g + u
                 nc.tensor.transpose(tpm[:, u, :], msd[:, yb * P : (yb + 1) * P], ident[:])
-            nc.vector.tensor_copy(out=maskp[:, 4 * g : 4 * g + 4, :], in_=tpm[:, :, 0:TAPS])
-
-        gg0 = keep.tile([P, 4 * B * L], BF16, name="gg0", align_bytes=64)
-        gg0v = gg0[:].rearrange("p (y b z j) -> p y b z j", b=2, z=32, j=4)
-        grawv = graw[:].rearrange("p b j (y z) -> p y b z j", z=32)
-
-        def g_regroup(eng_copy, b, h):
-            eng_copy(out=gg0v[:, 16 * h : 16 * h + 16, b], in_=grawv[:, 16 * h : 16 * h + 16, b])
-
-        def g_quant(k, h, src):
-            nc.vector.quantize_mx(
-                out=gcodes[k][:, 64 + 1024 * h : 64 + 1024 * (h + 1)].bitcast(E5),
-                scales=gsc[k][:, 64 + 1024 * h : 64 + 1024 * (h + 1)],
-                in_=src,
+            nc.vector.tensor_copy(
+                out=maskp[:, 4 * g : 4 * g + 4],
+                in_=tpm[:, :, 0:96].rearrange("p u (k r) -> p u k r", r=32)[:, :, :, 0:3],
             )
 
-        def g_prep(k):
-            if k == 1:
-                g_regroup(nc.vector.tensor_copy, 0, 0)
-                g_regroup(nc.vector.tensor_copy, 0, 1)
-                g_regroup(nc.scalar.copy, 1, 0)
-                g_regroup(nc.vector.tensor_copy, 1, 1)
-                for h in range(2):
-                    g_quant(1, h, gg0[:, 4096 * h : 4096 * (h + 1)])
-                return
-            shifted = []
-            for h in range(2):
-                gs = gsp.tile([P, 4096], BF16, tag="gs", name="gs", align_bytes=64)
-                if k == 0:
-                    nc.vector.tensor_copy(out=gs[:, 0:4092], in_=gg0[:, 4096 * h + 4 : 4096 * (h + 1)])
-                    edge = 31
-                else:
-                    nc.vector.tensor_copy(out=gs[:, 4:4096], in_=gg0[:, 4096 * h : 4096 * (h + 1) - 4])
-                    edge = 0
-                nc.vector.memset(gs[:].rearrange("p (g z j) -> p g z j", z=32, j=4)[:, :, edge, :], 0.0)
-                shifted.append(gs)
-            for h in range(2):
-                g_quant(k, h, shifted[h][:])
-
-        load = {"V": 4.0, "S": 4.0, "G": 10.0, "PE": 8.0}
-
-        def w_prep(k):
-            for q in range(4):
-                wg = wgp.tile([P, 3, 128, 4], BF16, tag="wg", name="wg", align_bytes=64)
-                if W_ENG[k][q] == "V":
-                    eng_copy = nc.vector.tensor_copy
-                    load["V"] += 0.97
-                else:
-                    eng_copy = nc.scalar.copy
-                    load["S"] += 1.74
-                load["V"] += 0.39
+        wg = {}
+        for k in K_ORDER:
+            wg[k] = keep.tile([P, 3, CIN, 4], BF16, name="wg%d" % k, align_bytes=64)
+        for q in range(4):
+            for k in K_ORDER:
+                eng_copy = nc.vector.tensor_copy if W_ENG[str(k)][q] == "V" else nc.scalar.copy
                 eng_copy(
-                    out=wg[:].rearrange("p t c j -> p c t j"),
+                    out=wg[k][:, :, q * 128 : (q + 1) * 128, :].rearrange("p t c j -> p c t j"),
                     in_=wraw[q][:].rearrange("p j (c i k) -> p c i k j", i=3, k=3)[:, :, :, k, :],
                 )
-                for t in range(3):
-                    c0 = (3 * t + k) * CIN + q * 128
-                    nc.vector.quantize_mx(
-                        out=wcodes[:, c0 : c0 + 128].bitcast(E4),
-                        scales=wsc[:, c0 : c0 + 128],
-                        in_=wg[:, t].rearrange("p c j -> p (c j)"),
-                    )
+        for k in K_ORDER:
+            for t in range(3):
+                tap = 3 * t + k
+                nc.vector.quantize_mx(
+                    out=wcodes[:, tap * CIN : (tap + 1) * CIN].bitcast(E4),
+                    scales=wsc[:, tap * CIN : (tap + 1) * CIN],
+                    in_=wg[k][:, t].rearrange("p c j -> p (c j)"),
+                )
 
-        chains = {}
+        tiles = {}
 
-        def one_bank(yb, tap):
-            dy, k = 1 - tap // 3, tap % 3
-            src = k if k in COPIES else 1
-            c0 = 64 + (2 * yb + dy) * 64
+        def one_bank(yb, k, i):
+            tap = 3 * i + k
+            c0 = 64 + (2 * yb + 1 - i) * 64
             ps = psum.tile([P, CIN], F32, tag="mx", name="ps")
             nc.tensor.matmul_mx(
                 out=ps[:],
-                lhsT=gcodes[src][:, c0 : c0 + P].bitcast(E5),
-                lhsT_scale=gsc[src][:, c0 : c0 + P],
+                lhsT=gcodes[:, c0 : c0 + P].bitcast(E5),
+                lhsT_scale=gsc[:, c0 : c0 + P],
                 rhs=wcodes[:, tap * CIN : (tap + 1) * CIN].bitcast(E4),
                 rhs_scale=wsc[:, tap * CIN : (tap + 1) * CIN],
                 start=True,
                 stop=True,
             )
-            m = maskp[:, yb, tap : tap + 1]
-            key = (yb, CHAIN[k])
-            if key not in chains:
-                chains[key] = {"v": None, "s": []}
-            ch = chains[key]
-            load["PE"] += T_PASS
-            ref = max(load["V"], load["S"])
-            how = "V"
-            if load["S"] + T_S <= load["V"] + T_V:
-                room = load["PE"] + T_TILE <= ref
-                if not ch["s"] and (ch["v"] is None or room):
-                    how = "S"
-                elif ch["s"] and max(load["G"], load["S"] + T_S) + T_G <= ref + G_SLACK:
-                    how = "G"
-                elif room:
-                    how = "S"
-            if how == "V":
-                load["V"] += T_V
-                if ch["v"] is not None:
-                    a = ch["v"]
-                    nc.vector.scalar_tensor_tensor(out=a[:], in0=ps[:], scalar=m, in1=a[:], op0=ALU.mult, op1=ALU.add)
-                elif ch["s"]:
-                    a = ch["s"].pop()
-                    ch["v"] = a
-                    nc.vector.scalar_tensor_tensor(out=a[:], in0=ps[:], scalar=m, in1=a[:], op0=ALU.mult, op1=ALU.add)
-                else:
-                    a = accp.tile([P, CIN], F32, tag="acc", name="acc")
-                    ch["v"] = a
-                    load["PE"] += T_TILE
-                    nc.vector.tensor_scalar(out=a[:], in0=ps[:], scalar1=m, scalar2=None, op0=ALU.mult)
-            elif how == "S":
-                load["S"] += T_S
-                load["PE"] += T_TILE
+            m = maskp[:, yb, k, i : i + 1]
+            if i == 0:
                 a = accp.tile([P, CIN], F32, tag="acc", name="acc")
-                ch["s"].append(a)
+                tiles[(yb, k)] = a
                 nc.scalar.activation(out=a[:], in_=ps[:], func=ACT.Copy, scale=m)
             else:
-                load["S"] += T_S
-                load["G"] = max(load["G"], load["S"]) + T_G
-                a = ch["s"][-1]
-                t = tmpp.tile([P, CIN], F32, tag="tmp", name="tmp")
-                nc.scalar.activation(out=t[:], in_=ps[:], func=ACT.Copy, scale=m)
-                nc.gpsimd.tensor_tensor(out=a[:], in0=a[:], in1=t[:], op=ALU.add)
+                a = tiles[(yb, k)]
+                nc.vector.scalar_tensor_tensor(out=a[:], in0=ps[:], scalar=m, in1=a[:], op0=ALU.mult, op1=ALU.add)
 
         def finish_pair(pr):
             ot = otp.tile([P, 4, 2, P], F32, tag="ot", name="ot")
             banks = []
             for hh in range(2):
                 yb = 2 * pr + hh
-                parts = []
-                for k in K_ORDER:
-                    key = (yb, CHAIN[k])
-                    if key in chains:
-                        ch = chains.pop(key)
-                        dz = 0 if k in COPIES else 1 - k
-                        tiles = ([ch["v"]] if ch["v"] is not None else []) + ch["s"]
-                        parts.extend([(a, perms[dz]) for a in tiles])
                 tp = psum_t.tile([P, 4, P], F32, tag="tp", name="tp")
                 for cb in range(4):
-                    for n, (a, pm) in enumerate(parts):
+                    for n, k in enumerate(K_ORDER):
                         nc.tensor.matmul(
                             out=tp[:, cb, :],
-                            lhsT=a[:, cb * P : (cb + 1) * P],
-                            rhs=pm[:],
+                            lhsT=tiles[(yb, k)][:, cb * P : (cb + 1) * P],
+                            rhs=perms[k][:],
                             is_transpose=True,
                             start=(n == 0),
-                            stop=(n == len(parts) - 1),
+                            stop=(n == 2),
                         )
                 banks.append(tp)
             for hh in range(2):
-                dst = ot[:, :, :, 64 * hh : 64 * hh + 64]
-                src = banks[hh][:].rearrange("p cb (b r) -> p cb b r", b=2)
-                if load["V"] + T_OUT < load["S"]:
-                    load["V"] += T_OUT
-                    nc.vector.tensor_copy(out=dst, in_=src)
-                else:
-                    load["S"] += T_OUT
-                    nc.scalar.copy(out=dst, in_=src)
+                nc.scalar.copy(
+                    out=ot[:, :, :, 64 * hh : 64 * hh + 64],
+                    in_=banks[hh][:].rearrange("p cb (b r) -> p cb b r", b=2),
+                )
             for b in range(B):
                 nc.sync.dma_start(
                     out=out[b].rearrange("(cb c) y z -> c cb (y z)", c=P)[:, :, pr * P : (pr + 1) * P],
                     in_=ot[:, :, b, :],
                 )
 
-        g_prep(1)
-        for k in K_ORDER:
-            if k in COPIES:
-                g_prep(k)
-                load["V"] += 3.84
-            w_prep(k)
-        for pr in range(NBLK // 2):
-            for k in K_ORDER:
-                for t in range(3):
-                    for hh in range(2):
-                        one_bank(2 * pr + hh, 3 * t + k)
-            finish_pair(pr)
+        steps = [(pr, k) for pr in range(NBLK // 2) for k in K_ORDER]
+        for hh in range(2):
+            one_bank(2 * steps[0][0] + hh, steps[0][1], 0)
+        for n, (pr, k) in enumerate(steps):
+            nxt = steps[n + 1] if n + 1 < len(steps) else None
+            if nxt is not None:
+                one_bank(2 * nxt[0], nxt[1], 0)
+            one_bank(2 * pr, k, 1)
+            one_bank(2 * pr + 1, k, 1)
+            if nxt is not None:
+                one_bank(2 * nxt[0] + 1, nxt[1], 0)
+            one_bank(2 * pr, k, 2)
+            one_bank(2 * pr + 1, k, 2)
+            if n % 3 == 0 and n > 0:
+                finish_pair(pr - 1)
+        finish_pair(NBLK // 2 - 1)

@@ -26,7 +26,7 @@ BYTES = 2 * (COUT * CIN * TAPS + B * COUT * L + TAPS * L) + 4 * B * CIN * L
 
 K_ORDER = (1, 0, 2)
 W_ENG = {"0":"SSSS","1":"VVVV","2":"VSVS"}
-PIN = False
+PIN = True
 
 
 def tile_input_masked_conv2d_kernel(tc, x, mask, weight, bias, grad_out, out):

@@ -26,7 +26,8 @@ BYTES = 2 * (COUT * CIN * TAPS + B * COUT * L + TAPS * L) + 4 * B * CIN * L
 
 K_ORDER = (1, 0, 2)
 W_ENG = {"0":"SSSS","1":"VVVV","2":"VSVS"}
-PIN = True
+PIN = False
+G_TAPS = (2,)
 
 
 def tile_input_masked_conv2d_kernel(tc, x, mask, weight, bias, grad_out, out):
@@ -36,7 +37,8 @@ def tile_input_masked_conv2d_kernel(tc, x, mask, weight, bias, grad_out, out):
             ctx.enter_context(tc.manual_schedule())
         keep = ctx.enter_context(tc.tile_pool(name="keep", bufs=1))
         otp = ctx.enter_context(tc.tile_pool(name="otp", bufs=3))
-        accp = ctx.enter_context(tc.tile_pool(name="accp", bufs=16))
+        tmpp = ctx.enter_context(tc.tile_pool(name="tmpp", bufs=4))
+        accp = ctx.enter_context(tc.tile_pool(name="accp", bufs=18))
         psum = ctx.enter_context(tc.psum_pool(name="psum", bufs=6))
         psum_t = ctx.enter_context(tc.psum_pool(name="psum_t", bufs=2))
 
@@ -161,6 +163,11 @@ def tile_input_masked_conv2d_kernel(tc, x, mask, weight, bias, grad_out, out):
                 a = accp.tile([P, CIN], F32, tag="acc", name="acc")
                 tiles[(yb, k)] = a
                 nc.scalar.activation(out=a[:], in_=ps[:], func=ACT.Copy, scale=m)
+            elif i == 1 and k in G_TAPS:
+                a = tiles[(yb, k)]
+                t = tmpp.tile([P, CIN], F32, tag="tmp", name="tmp")
+                nc.scalar.activation(out=t[:], in_=ps[:], func=ACT.Copy, scale=m)
+                nc.gpsimd.tensor_tensor(out=a[:], in0=a[:], in1=t[:], op=ALU.add)
             else:
                 a = tiles[(yb, k)]
                 nc.vector.scalar_tensor_tensor(out=a[:], in0=ps[:], scalar=m, in1=a[:], op0=ALU.mult, op1=ALU.add)
@@ -194,16 +201,23 @@ def tile_input_masked_conv2d_kernel(tc, x, mask, weight, bias, grad_out, out):
                 )
 
         steps = [(pr, k) for pr in range(NBLK // 2) for k in K_ORDER]
+
+        def start_chain(yb, k):
+            one_bank(yb, k, 0)
+            if k in G_TAPS:
+                one_bank(yb, k, 1)
+
         for hh in range(2):
-            one_bank(2 * steps[0][0] + hh, steps[0][1], 0)
+            start_chain(2 * steps[0][0] + hh, steps[0][1])
         for n, (pr, k) in enumerate(steps):
             nxt = steps[n + 1] if n + 1 < len(steps) else None
             if nxt is not None:
-                one_bank(2 * nxt[0], nxt[1], 0)
-            one_bank(2 * pr, k, 1)
-            one_bank(2 * pr + 1, k, 1)
+                start_chain(2 * nxt[0], nxt[1])
+            if k not in G_TAPS:
+                one_bank(2 * pr, k, 1)
+                one_bank(2 * pr + 1, k, 1)
             if nxt is not None:
-                one_bank(2 * nxt[0] + 1, nxt[1], 0)
+                start_chain(2 * nxt[0] + 1, nxt[1])
             one_bank(2 * pr, k, 2)
             one_bank(2 * pr + 1, k, 2)
             if n % 3 == 0 and n > 0:

@@ -27,7 +27,6 @@ BYTES = 2 * (COUT * CIN * TAPS + B * COUT * L + TAPS * L) + 4 * B * CIN * L
 K_ORDER = (1, 0, 2)
 W_ENG = {"0":"SSSS","1":"VVVV","2":"VSVS"}
 PIN = False
-G_TAPS = (2,)
 
 
 def tile_input_masked_conv2d_kernel(tc, x, mask, weight, bias, grad_out, out):
@@ -37,8 +36,7 @@ def tile_input_masked_conv2d_kernel(tc, x, mask, weight, bias, grad_out, out):
             ctx.enter_context(tc.manual_schedule())
         keep = ctx.enter_context(tc.tile_pool(name="keep", bufs=1))
         otp = ctx.enter_context(tc.tile_pool(name="otp", bufs=3))
-        tmpp = ctx.enter_context(tc.tile_pool(name="tmpp", bufs=4))
-        accp = ctx.enter_context(tc.tile_pool(name="accp", bufs=18))
+        accp = ctx.enter_context(tc.tile_pool(name="accp", bufs=16))
         psum = ctx.enter_context(tc.psum_pool(name="psum", bufs=6))
         psum_t = ctx.enter_context(tc.psum_pool(name="psum_t", bufs=2))
 
@@ -163,11 +161,6 @@ def tile_input_masked_conv2d_kernel(tc, x, mask, weight, bias, grad_out, out):
                 a = accp.tile([P, CIN], F32, tag="acc", name="acc")
                 tiles[(yb, k)] = a
                 nc.scalar.activation(out=a[:], in_=ps[:], func=ACT.Copy, scale=m)
-            elif i == 1 and k in G_TAPS:
-                a = tiles[(yb, k)]
-                t = tmpp.tile([P, CIN], F32, tag="tmp", name="tmp")
-                nc.scalar.activation(out=t[:], in_=ps[:], func=ACT.Copy, scale=m)
-                nc.gpsimd.tensor_tensor(out=a[:], in0=a[:], in1=t[:], op=ALU.add)
             else:
                 a = tiles[(yb, k)]
                 nc.vector.scalar_tensor_tensor(out=a[:], in0=ps[:], scalar=m, in1=a[:], op0=ALU.mult, op1=ALU.add)
@@ -200,26 +193,20 @@ def tile_input_masked_conv2d_kernel(tc, x, mask, weight, bias, grad_out, out):
                     in_=ot[:, :, b, :],
                 )
 
-        steps = [(pr, k) for pr in range(NBLK // 2) for k in K_ORDER]
-
-        def start_chain(yb, k):
-            one_bank(yb, k, 0)
-            if k in G_TAPS:
-                one_bank(yb, k, 1)
-
-        for hh in range(2):
-            start_chain(2 * steps[0][0] + hh, steps[0][1])
-        for n, (pr, k) in enumerate(steps):
-            nxt = steps[n + 1] if n + 1 < len(steps) else None
-            if nxt is not None:
-                start_chain(2 * nxt[0], nxt[1])
-            if k not in G_TAPS:
+        with tc.manual_schedule():
+            steps = [(pr, k) for pr in range(NBLK // 2) for k in K_ORDER]
+            for hh in range(2):
+                one_bank(2 * steps[0][0] + hh, steps[0][1], 0)
+            for n, (pr, k) in enumerate(steps):
+                nxt = steps[n + 1] if n + 1 < len(steps) else None
+                if nxt is not None:
+                    one_bank(2 * nxt[0], nxt[1], 0)
                 one_bank(2 * pr, k, 1)
                 one_bank(2 * pr + 1, k, 1)
-            if nxt is not None:
-                start_chain(2 * nxt[0] + 1, nxt[1])
-            one_bank(2 * pr, k, 2)
-            one_bank(2 * pr + 1, k, 2)
-            if n % 3 == 0 and n > 0:
-                finish_pair(pr - 1)
-        finish_pair(NBLK // 2 - 1)
+                if nxt is not None:
+                    one_bank(2 * nxt[0] + 1, nxt[1], 0)
+                one_bank(2 * pr, k, 2)
+                one_bank(2 * pr + 1, k, 2)
+                if n % 3 == 0 and n > 0:
+                    finish_pair(pr - 1)
+            finish_pair(NBLK // 2 - 1)

from contextlib import ExitStack

import concourse.bass as bass
import concourse.mybir as mybir
import concourse.tile as tile
from concourse.masks import make_identity

F32 = mybir.dt.float32
BF16 = mybir.dt.bfloat16
U32 = mybir.dt.uint32
U8 = mybir.dt.uint8
I32 = mybir.dt.int32
E4 = mybir.dt.float8_e4m3fn_x4
E5 = mybir.dt.float8_e5m2_x4
ALU = mybir.AluOpType
ACT = mybir.ActivationFunctionType

P = 128
B, CIN, COUT, H, W = 2, 512, 512, 32, 32
L = H * W
TAPS = 9
NBLK = 16
GCOLS = 64 * (H + 2)
FLOPS = 2 * COUT * CIN * TAPS * B * L
BYTES = 2 * (COUT * CIN * TAPS + B * COUT * L + TAPS * L) + 4 * B * CIN * L

K_ORDER = (1, 0, 2)
W_ENG = {"0":"SSSS","1":"VVVV","2":"VSVS"}
PIN = False


def tile_input_masked_conv2d_kernel(tc, x, mask, weight, bias, grad_out, out):
    nc = tc.nc
    with ExitStack() as ctx:
        if PIN:
            ctx.enter_context(tc.manual_schedule())
        keep = ctx.enter_context(tc.tile_pool(name="keep", bufs=1))
        otp = ctx.enter_context(tc.tile_pool(name="otp", bufs=3))
        accp = ctx.enter_context(tc.tile_pool(name="accp", bufs=16))
        psum = ctx.enter_context(tc.psum_pool(name="psum", bufs=6))
        psum_t = ctx.enter_context(tc.psum_pool(name="psum_t", bufs=2))

        ms = keep.tile([P, L], BF16, name="ms")
        nc.vector.memset(ms[:], 0.0)
        graw = keep.tile([P, B, 4, L], BF16, name="graw")
        for b in range(B):
            nc.sync.dma_start(out=graw[:, b], in_=grad_out[b].rearrange("(p j) y z -> p j (y z)", j=4))
        for i in range(3):
            dy = 1 - i
            d0, s0, n = max(0, -32 * dy), max(0, 32 * dy), L - 32 * abs(dy)
            nc.scalar.dma_start(out=ms[i:96:32, d0 : d0 + n], in_=mask[0, 3 * i : 3 * i + 3, s0 : s0 + n])
        wview = weight.rearrange("(p j) c i k -> p j (c i k)", j=4)
        wraw = []
        for q in range(4):
            wr = keep.tile([P, 4, 128 * TAPS], BF16, name="wraw%d" % q)
            nc.sync.dma_start(out=wr[:], in_=wview[:, :, q * 1152 : (q + 1) * 1152])
            wraw.append(wr)

        ident = keep.tile([P, P], F32, name="ident")
        make_identity(nc, ident[:])
        iv = ident[:].rearrange("p (d b z) -> p b d z", b=2, d=2)
        perms = {}
        for k in K_ORDER:
            pm = keep.tile([P, P], F32, name="perm%d" % k)
            pv = pm[:].rearrange("p (b d z) -> p b d z", b=2, d=2)
            if k == 1:
                nc.vector.tensor_copy(out=pv, in_=iv)
            elif k == 0:
                nc.vector.tensor_copy(out=pv[:, :, :, 0:31], in_=iv[:, :, :, 1:32])
                nc.vector.tensor_copy(out=pv[:, :, :, 31:32], in_=iv[:, :, :, 0:1])
            else:
                nc.vector.tensor_copy(out=pv[:, :, :, 1:32], in_=iv[:, :, :, 0:31])
                nc.vector.tensor_copy(out=pv[:, :, :, 0:1], in_=iv[:, :, :, 31:32])
            perms[k] = pm

        gcodes = keep.tile([P, GCOLS], U32, name="gcodes", align_bytes=64)
        gsc = keep.tile([P, GCOLS], U8, name="gsc", align_bytes=64)
        for c0 in (0, GCOLS - 64):
            nc.vector.memset(gcodes[:, c0 : c0 + 64].bitcast(I32), 0)
            nc.vector.memset(gsc[:, c0 : c0 + 64].bitcast(I32), 0)
        wcodes = keep.tile([P, TAPS * CIN], U32, name="wcodes", align_bytes=64)
        wsc = keep.tile([P, TAPS * CIN], U8, name="wsc", align_bytes=64)

        msv = ms[:].rearrange("r (y z) -> r y z", z=32)
        nc.gpsimd.memset(msv[0:3, :, 0:1], 0.0)
        nc.gpsimd.memset(msv[64:67, :, 31:32], 0.0)
        msd = keep.tile([P, NBLK * P], F32, name="msd")
        nc.gpsimd.tensor_scalar(
            out=msd[:].rearrange("r (y b z) -> r y b z", b=2, z=32),
            in0=msv.unsqueeze(2).to_broadcast([P, H, 2, W]),
            scalar1=1.0,
            scalar2=0.0,
            op0=ALU.mult,
            op1=ALU.add,
        )

        gg0 = keep.tile([P, 4 * B * L], BF16, name="gg0", align_bytes=64)
        gg0v = gg0[:].rearrange("p (y b z j) -> p y b z j", b=2, z=32, j=4)
        grawv = graw[:].rearrange("p b j (y z) -> p y b z j", z=32)
        for eng_copy, b, h in (
            (nc.vector.tensor_copy, 0, 0),
            (nc.vector.tensor_copy, 0, 1),
            (nc.scalar.copy, 1, 0),
            (nc.vector.tensor_copy, 1, 1),
        ):
            eng_copy(out=gg0v[:, 16 * h : 16 * h + 16, b], in_=grawv[:, 16 * h : 16 * h + 16, b])
        for h in range(2):
            nc.vector.quantize_mx(
                out=gcodes[:, 64 + 1024 * h : 64 + 1024 * (h + 1)].bitcast(E5),
                scales=gsc[:, 64 + 1024 * h : 64 + 1024 * (h + 1)],
                in_=gg0[:, 4096 * h : 4096 * (h + 1)],
            )

        maskp = keep.tile([P, NBLK, 3, 3], F32, name="maskp")
        for g in range(4):
            tpm = psum_t.tile([P, 4, P], F32, tag="tp", name="tpm")
            for u in range(4):
                yb = 4 * g + u
                nc.tensor.transpose(tpm[:, u, :], msd[:, yb * P : (yb + 1) * P], ident[:])
            nc.vector.tensor_copy(
                out=maskp[:, 4 * g : 4 * g + 4],
                in_=tpm[:, :, 0:96].rearrange("p u (k r) -> p u k r", r=32)[:, :, :, 0:3],
            )

        wg = {}
        for k in K_ORDER:
            wg[k] = keep.tile([P, 3, CIN, 4], BF16, name="wg%d" % k, align_bytes=64)
        for q in range(4):
            for k in K_ORDER:
                eng_copy = nc.vector.tensor_copy if W_ENG[str(k)][q] == "V" else nc.scalar.copy
                eng_copy(
                    out=wg[k][:, :, q * 128 : (q + 1) * 128, :].rearrange("p t c j -> p c t j"),
                    in_=wraw[q][:].rearrange("p j (c i k) -> p c i k j", i=3, k=3)[:, :, :, k, :],
                )
        for k in K_ORDER:
            for t in range(3):
                tap = 3 * t + k
                nc.vector.quantize_mx(
                    out=wcodes[:, tap * CIN : (tap + 1) * CIN].bitcast(E4),
                    scales=wsc[:, tap * CIN : (tap + 1) * CIN],
                    in_=wg[k][:, t].rearrange("p c j -> p (c j)"),
                )

        tiles = {}

        def one_bank(yb, k, i):
            tap = 3 * i + k
            c0 = 64 + (2 * yb + 1 - i) * 64
            ps = psum.tile([P, CIN], F32, tag="mx", name="ps")
            nc.tensor.matmul_mx(
                out=ps[:],
                lhsT=gcodes[:, c0 : c0 + P].bitcast(E5),
                lhsT_scale=gsc[:, c0 : c0 + P],
                rhs=wcodes[:, tap * CIN : (tap + 1) * CIN].bitcast(E4),
                rhs_scale=wsc[:, tap * CIN : (tap + 1) * CIN],
                start=True,
                stop=True,
            )
            m = maskp[:, yb, k, i : i + 1]
            if i == 0:
                a = accp.tile([P, CIN], F32, tag="acc", name="acc")
                tiles[(yb, k)] = a
                nc.scalar.activation(out=a[:], in_=ps[:], func=ACT.Copy, scale=m)
            else:
                a = tiles[(yb, k)]
                nc.vector.scalar_tensor_tensor(out=a[:], in0=ps[:], scalar=m, in1=a[:], op0=ALU.mult, op1=ALU.add)

        def finish_pair(pr):
            ot = otp.tile([P, 4, 2, P], F32, tag="ot", name="ot")
            banks = []
            for hh in range(2):
                yb = 2 * pr + hh
                tp = psum_t.tile([P, 4, P], F32, tag="tp", name="tp")
                for cb in range(4):
                    for n, k in enumerate(K_ORDER):
                        nc.tensor.matmul(
                            out=tp[:, cb, :],
                            lhsT=tiles[(yb, k)][:, cb * P : (cb + 1) * P],
                            rhs=perms[k][:],
                            is_transpose=True,
                            start=(n == 0),
                            stop=(n == 2),
                        )
                banks.append(tp)
            for hh in range(2):
                nc.scalar.copy(
                    out=ot[:, :, :, 64 * hh : 64 * hh + 64],
                    in_=banks[hh][:].rearrange("p cb (b r) -> p cb b r", b=2),
                )
            for b in range(B):
                nc.sync.dma_start(
                    out=out[b].rearrange("(cb c) y z -> c cb (y z)", c=P)[:, :, pr * P : (pr + 1) * P],
                    in_=ot[:, :, b, :],
                )

        with tc.manual_schedule():
            steps = [(pr, k) for pr in range(NBLK // 2) for k in K_ORDER]
            for hh in range(2):
                one_bank(2 * steps[0][0] + hh, steps[0][1], 0)
            for n, (pr, k) in enumerate(steps):
                nxt = steps[n + 1] if n + 1 < len(steps) else None
                if nxt is not None:
                    one_bank(2 * nxt[0], nxt[1], 0)
                one_bank(2 * pr, k, 1)
                one_bank(2 * pr + 1, k, 1)
                if nxt is not None:
                    one_bank(2 * nxt[0] + 1, nxt[1], 0)
                one_bank(2 * pr, k, 2)
                one_bank(2 * pr + 1, k, 2)
                if n % 3 == 0 and n > 0:
                    finish_pair(pr - 1)
            finish_pair(NBLK // 2 - 1)
